import numpy as np
import ml_dtypes


def mxq(x, axis, fmt="e4m3"):
    dtype, down = {"e4m3": (ml_dtypes.float8_e4m3fn, 7), "e5m2": (ml_dtypes.float8_e5m2, 14)}[fmt]
    v = np.moveaxis(np.asarray(x, np.float32).astype(ml_dtypes.bfloat16).astype(np.float64), axis, -1)
    blocks = v.reshape(v.shape[:-1] + (-1, 32))
    amax = np.abs(blocks).max(-1, keepdims=True)
    byte = np.maximum(np.where(amax > 0, np.frexp(amax)[1] - 1 + 127, 0) - down, 1)
    scale = np.exp2(byte - 127.0)
    codes = (blocks / scale).astype(np.float32).astype(dtype).astype(np.float64)
    return np.moveaxis((codes * scale).reshape(v.shape), -1, axis)


WIDE = False


def mx_kscale(k):
    if not WIDE:
        return np.ones(k)
    levels = np.array([10, -10, 5, -5, 0])
    if k % 512:
        return np.exp2(np.random.permutation(np.resize(levels, k // 32))).repeat(32)
    a = np.empty((k // 512, 16))
    for p in range(k // 512):
        a[p, :8] = np.random.permutation(np.resize(levels, 8))
        for g in range(8):
            far = levels[np.abs(levels - a[p, g]) >= 10]
            a[p, g + 8] = far[np.random.randint(len(far))]
    return np.exp2(a.ravel()).repeat(32)


BF16 = ml_dtypes.bfloat16


def bf(x):
    return np.asarray(x, np.float32).astype(BF16)


def f64(x):
    return np.asarray(x).astype(np.float64)


B, CIN, H, W, CP, G = 3, 2048, 16, 16, 1024, 2
CG = CP // G
HW = H * W
ATT_N = np.sqrt(HW * HW * CG / CIN + HW * CG)


def setup_inputs():
    s = mx_kscale(CIN)
    r = np.sqrt(2.5 / ATT_N) / np.sqrt(CIN)
    return {"x": bf(np.random.standard_normal((B, CIN, H, W)) * s[None, :, None, None]),
            "Wt": bf(np.random.standard_normal((CP, CIN)) / np.sqrt(CIN) / s),
            "Wp": bf(np.random.standard_normal((CP, CIN)) * r / s),
            "Wg": bf(np.random.standard_normal((CP, CIN)) * r / s)}


def reference(x, Wt, Wp, Wg):
    xq = mxq(f64(x).reshape(B, CIN, HW), 1, "e4m3")
    t = mxq(f64(Wt), 1, "e4m3") @ xq
    p = mxq(f64(Wp), 1, "e4m3") @ xq
    g = mxq(f64(Wg), 1, "e4m3") @ xq
    t = t.reshape(B, G, CG * HW)
    p = p.reshape(B, G, CG * HW)
    g = g.reshape(B, G, CG * HW)
    att = (p * g).sum(-1, keepdims=True)
    return (att * t).reshape(B, G, CG, HW)

@@ -1,0 +1,219 @@
+from contextlib import ExitStack
+
+import concourse.mybir as mybir
+from concourse.masks import make_identity
+
+F32 = mybir.dt.float32
+BF16 = mybir.dt.bfloat16
+U32 = mybir.dt.uint32
+U8 = mybir.dt.uint8
+FP8X4 = mybir.dt.float8_e4m3fn_x4
+MULT = mybir.AluOpType.mult
+ADD = mybir.AluOpType.add
+COPY = mybir.ActivationFunctionType.Copy
+
+P = 128
+PACK = 4
+BANK = 512
+IMAGES = 3
+CIN = 2048
+HW = 256
+CP = 1024
+GROUPS = 2
+PASSES = CIN // (P * PACK)
+PANELS = CP // P
+PPG = PANELS // GROUPS
+PG_PAIRS = PANELS
+T_PAIRS = PANELS // 2
+PAIRS = PG_PAIRS + T_PAIRS
+START_PAIRS = IMAGES
+
+FLOPS = 2 * 3 * CP * CIN * IMAGES * HW
+
+
+def tile_spatialcgnl_pa_kernel(tc, x, Wt, Wp, Wg, out):
+    nc = tc.nc
+    with ExitStack() as ctx:
+        const = ctx.enter_context(tc.tile_pool(name="const", bufs=1))
+        xraw_pool = ctx.enter_context(tc.tile_pool(name="xraw", bufs=IMAGES))
+        xgrp_pool = ctx.enter_context(tc.tile_pool(name="xgrp", bufs=2))
+        wraw_pool = ctx.enter_context(tc.tile_pool(name="wraw", bufs=2 * PAIRS))
+        wgrp_pool = ctx.enter_context(tc.tile_pool(name="wgrp", bufs=4))
+        wq_pool = ctx.enter_context(tc.tile_pool(name="wq", bufs=10))
+        small = ctx.enter_context(tc.tile_pool(name="small", bufs=4))
+        tp_pool = ctx.enter_context(tc.psum_pool(name="tp", bufs=4))
+        acc_pool = ctx.enter_context(tc.psum_pool(name="acc", bufs=4))
+        ctx.enter_context(tc.manual_schedule())
+
+        def panel_in_dram(j, s):
+            if j < PG_PAIRS:
+                w, panel = (Wp, Wg)[s], j
+            else:
+                w, panel = Wt, 2 * (j - PG_PAIRS) + s
+            view = w.rearrange("(c p a) k -> c a p k", c=GROUPS, p=P, a=PPG)
+            return view[panel // PPG, panel % PPG]
+
+        xraw = [xraw_pool.tile([P, PASSES, PACK, HW], BF16, name="xraw%d" % b, tag="xraw") for b in range(IMAGES)]
+        wraw = [
+            [wraw_pool.tile([P, CIN], BF16, name="wraw%d_%d" % (j, s), tag="wraw") for s in range(2)]
+            for j in range(PAIRS)
+        ]
+
+        def load_x(b):
+            src = x[b].rearrange("(g p t) h w -> p g (t h w)", g=PASSES, p=P, t=PACK)
+            dst = xraw[b][:].rearrange("p g t n -> p g (t n)")
+            for half in range(2):
+                chunks = slice(2 * half, 2 * half + 2)
+                nc.sync.dma_start(out=dst[:, chunks, :], in_=src[:, chunks, :])
+
+        def load_w(j):
+            for s in range(2):
+                nc.sync.dma_start(out=wraw[j][s][:], in_=panel_in_dram(j, s))
+
+        for j in range(PAIRS):
+            load_w(j)
+            if j < START_PAIRS:
+                load_x(j)
+
+        ident = const.tile([P, P], F32)
+        make_identity(nc, ident[:])
+        ones = const.tile([P, P], F32)
+        nc.vector.memset(ones[:], 1.0)
+        part = const.tile([P, PG_PAIRS * IMAGES], F32)
+        att = const.tile([P, GROUPS * IMAGES], F32)
+        xc = [const.tile([P, PASSES * HW], U32, name="xc%d" % b, align_bytes=64) for b in range(IMAGES)]
+        xs = [const.tile([P, PASSES * HW], U8, name="xs%d" % b, align_bytes=64) for b in range(IMAGES)]
+
+        wc = {}
+        ws = {}
+        wgrp = {}
+        acc = {}
+
+        def prep_x(b):
+            xgrp = xgrp_pool.tile([P, PASSES, HW, PACK], BF16, name="xgrp%d" % b, tag="xgrp", align_bytes=64)
+
+            def regroup(engine_copy, g):
+                engine_copy(
+                    out=xgrp[:, g].rearrange("p (v f) t -> p v t f", f=4),
+                    in_=xraw[b][:, g].rearrange("p t (v f) -> p v t f", f=4),
+                )
+
+            def quantise(half):
+                cols = slice(2 * HW * half, 2 * HW * half + 2 * HW)
+                nc.vector.quantize_mx(
+                    out=xc[b][:, cols].bitcast(FP8X4),
+                    scales=xs[b][:, cols],
+                    in_=xgrp[:, 2 * half : 2 * half + 2].rearrange("p g n t -> p (g n t)"),
+                )
+
+            regroup(nc.vector.tensor_copy, 0)
+            regroup(nc.vector.tensor_copy, 1)
+            regroup(nc.scalar.copy, 3)
+            regroup(nc.vector.tensor_copy, 2)
+            quantise(0)
+            quantise(1)
+
+        def transposes(j):
+            for s in range(2):
+                words = wraw[j][s][:].bitcast(F32)
+                regrouped = wgrp_pool.tile([P, CIN], BF16, name="wgrp%d_%d" % (j, s), tag="wgrp", align_bytes=64)
+                wgrp[(j, s)] = regrouped
+                for half in range(2):
+                    tp = tp_pool.tile([P, 4, P], F32, name="tp%d_%d_%d" % (j, s, half), tag="tp")
+                    for slot in range(4):
+                        g, u = 2 * half + slot // 2, slot % 2
+                        cols = words[:, 2 * P * g + u : 2 * P * g + 2 * P : 2]
+                        nc.tensor.transpose(tp[:, slot, :], cols, ident[:])
+                    nc.scalar.copy(
+                        out=regrouped[:].bitcast(F32)[:, BANK * half : BANK * half + BANK].rearrange(
+                            "p (g m u) -> p g m u", g=2, m=P, u=2
+                        ),
+                        in_=tp[:].rearrange("p (g u) m -> p g m u", g=2, u=2),
+                    )
+
+        def quantise_w(j):
+            for s in range(2):
+                wc[(j, s)] = wq_pool.tile([P, PASSES * P], U32, name="wc%d_%d" % (j, s), tag="wc", align_bytes=64)
+                ws[(j, s)] = wq_pool.tile([P, PASSES * P], U8, name="ws%d_%d" % (j, s), tag="ws", align_bytes=64)
+                nc.vector.quantize_mx(
+                    out=wc[(j, s)][:].bitcast(FP8X4), scales=ws[(j, s)][:], in_=wgrp[(j, s)][:]
+                )
+
+        def job(j, b):
+            bank = acc_pool.tile([P, 2, HW], F32, name="acc%d_%d" % (j, b), tag="acc")
+            acc[(j, b)] = bank
+            for s in range(2):
+                for g in range(PASSES):
+                    nc.tensor.matmul_mx(
+                        out=bank[:, s, :],
+                        lhsT=wc[(j, s)][:, P * g : P * g + P].bitcast(FP8X4),
+                        lhsT_scale=ws[(j, s)][:, P * g : P * g + P],
+                        rhs=xc[b][:, HW * g : HW * g + HW].bitcast(FP8X4),
+                        rhs_scale=xs[b][:, HW * g : HW * g + HW],
+                        start=(g == 0),
+                        stop=(g == PASSES - 1),
+                    )
+
+        def drain(j, b):
+            bank = acc[(j, b)]
+            if j < PG_PAIRS:
+                p_sb = small.tile([P, HW], F32, name="p_sb%d_%d" % (j, b), tag="p_sb")
+                nc.scalar.copy(out=p_sb[:], in_=bank[:, 0, :])
+                prod = small.tile([P, HW], F32, name="prod%d_%d" % (j, b), tag="prod")
+                nc.vector.scalar_tensor_tensor(
+                    out=prod[:],
+                    in0=bank[:, 1, :],
+                    scalar=1.0,
+                    in1=p_sb[:],
+                    op0=MULT,
+                    op1=MULT,
+                    accum_out=part[:, j * IMAGES + b : j * IMAGES + b + 1],
+                )
+            else:
+                panel = 2 * (j - PG_PAIRS)
+                c, a = panel // PPG, panel % PPG
+                factor = att[:, c * IMAGES + b : c * IMAGES + b + 1]
+                y_sb = small.tile([P, 2, HW], F32, name="y_sb%d_%d" % (j, b), tag="y_sb")
+                if b == 1:
+                    nc.scalar.activation(out=y_sb[:], in_=bank[:], func=COPY, scale=factor)
+                else:
+                    nc.vector.tensor_scalar(out=y_sb[:], in0=bank[:], scalar1=factor, scalar2=None, op0=MULT)
+                dst = out[b, c].rearrange("(p a) n -> p a n", a=PPG)
+                nc.sync.dma_start(out=dst[:, a : a + 2, :], in_=y_sb[:])
+
+        def attention():
+            att_ps = tp_pool.tile([P, 4, P], F32, name="att_ps", tag="tp")
+            sums = att_ps[:, 0, 0 : PG_PAIRS * IMAGES]
+            nc.tensor.matmul(sums, lhsT=ones[:], rhs=part[:], start=True, stop=True)
+            nc.vector.tensor_reduce(
+                out=att[:].rearrange("p (c b) -> p c b", c=GROUPS),
+                in_=sums.rearrange("p (c a b) -> p c b a", c=GROUPS, a=PPG, b=IMAGES),
+                axis=mybir.AxisListType.X,
+                op=ADD,
+            )
+
+        def run(jobs, between=None):
+            for j, b in jobs:
+                job(j, b)
+            if between is not None:
+                prep_x(between)
+            for j, b in jobs:
+                drain(j, b)
+
+        transposes(0)
+        quantise_w(0)
+        prep_x(0)
+        for r in range(1, START_PAIRS + 1):
+            transposes(r)
+            quantise_w(r)
+            run([(j, r - 1) for j in range(r)], between=(r if r < IMAGES else None))
+            if r < START_PAIRS:
+                run([(r, b) for b in range(r)])
+        for j in range(START_PAIRS, PAIRS):
+            if j + 1 < PAIRS:
+                transposes(j + 1)
+                if j == PG_PAIRS:
+                    attention()
+                quantise_w(j + 1)
+            for b in range(IMAGES):
+                run([(j, b)])

@@ -27,6 +27,7 @@ PG_PAIRS = PANELS
 T_PAIRS = PANELS // 2
 PAIRS = PG_PAIRS + T_PAIRS
 START_PAIRS = IMAGES
+SORT_FROM = START_PAIRS + 1
 
 FLOPS = 2 * 3 * CP * CIN * IMAGES * HW
 
@@ -38,6 +39,7 @@ def tile_spatialcgnl_pa_kernel(tc, x, Wt, Wp, Wg, out):
         xraw_pool = ctx.enter_context(tc.tile_pool(name="xraw", bufs=IMAGES))
         xgrp_pool = ctx.enter_context(tc.tile_pool(name="xgrp", bufs=2))
         wraw_pool = ctx.enter_context(tc.tile_pool(name="wraw", bufs=2 * PAIRS))
+        wsort_pool = ctx.enter_context(tc.tile_pool(name="wsort", bufs=4))
         wgrp_pool = ctx.enter_context(tc.tile_pool(name="wgrp", bufs=4))
         wq_pool = ctx.enter_context(tc.tile_pool(name="wq", bufs=10))
         small = ctx.enter_context(tc.tile_pool(name="small", bufs=4))
@@ -86,6 +88,7 @@ def tile_spatialcgnl_pa_kernel(tc, x, Wt, Wp, Wg, out):
 
         wc = {}
         ws = {}
+        wsort = {}
         wgrp = {}
         acc = {}
 
@@ -113,6 +116,14 @@ def tile_spatialcgnl_pa_kernel(tc, x, Wt, Wp, Wg, out):
             quantise(0)
             quantise(1)
 
+        def sort_words(j):
+            for s in range(2):
+                wsort[(j, s)] = wsort_pool.tile([P, PASSES, 2, P], F32, name="wsort%d_%d" % (j, s), tag="wsort")
+                nc.vector.tensor_copy(
+                    out=wsort[(j, s)][:],
+                    in_=wraw[j][s][:].bitcast(F32).rearrange("p (g c u) -> p g u c", g=PASSES, u=2),
+                )
+
         def transposes(j):
             for s in range(2):
                 words = wraw[j][s][:].bitcast(F32)
@@ -122,7 +133,10 @@ def tile_spatialcgnl_pa_kernel(tc, x, Wt, Wp, Wg, out):
                     tp = tp_pool.tile([P, 4, P], F32, name="tp%d_%d_%d" % (j, s, half), tag="tp")
                     for slot in range(4):
                         g, u = 2 * half + slot // 2, slot % 2
-                        cols = words[:, 2 * P * g + u : 2 * P * g + 2 * P : 2]
+                        if j < SORT_FROM:
+                            cols = words[:, 2 * P * g + u : 2 * P * g + 2 * P : 2]
+                        else:
+                            cols = wsort[(j, s)][:, g, u, :]
                         nc.tensor.transpose(tp[:, slot, :], cols, ident[:])
                     nc.scalar.copy(
                         out=regrouped[:].bitcast(F32)[:, BANK * half : BANK * half + BANK].rearrange(
@@ -174,7 +188,7 @@ def tile_spatialcgnl_pa_kernel(tc, x, Wt, Wp, Wg, out):
                 c, a = panel // PPG, panel % PPG
                 factor = att[:, c * IMAGES + b : c * IMAGES + b + 1]
                 y_sb = small.tile([P, 2, HW], F32, name="y_sb%d_%d" % (j, b), tag="y_sb")
-                if b == 1:
+                if b != 1:
                     nc.scalar.activation(out=y_sb[:], in_=bank[:], func=COPY, scale=factor)
                 else:
                     nc.vector.tensor_scalar(out=y_sb[:], in0=bank[:], scalar1=factor, scalar2=None, op0=MULT)
@@ -209,11 +223,14 @@ def tile_spatialcgnl_pa_kernel(tc, x, Wt, Wp, Wg, out):
             run([(j, r - 1) for j in range(r)], between=(r if r < IMAGES else None))
             if r < START_PAIRS:
                 run([(r, b) for b in range(r)])
+        sort_words(SORT_FROM)
         for j in range(START_PAIRS, PAIRS):
             if j + 1 < PAIRS:
                 transposes(j + 1)
                 if j == PG_PAIRS:
                     attention()
+                if j + 2 < PAIRS:
+                    sort_words(j + 2)
                 quantise_w(j + 1)
             for b in range(IMAGES):
                 run([(j, b)])

@@ -220,10 +220,11 @@ def tile_spatialcgnl_pa_kernel(tc, x, Wt, Wp, Wg, out):
         for r in range(1, START_PAIRS + 1):
             transposes(r)
             quantise_w(r)
+            if r >= SORT_FROM - 1:
+                sort_words(r + 1)
             run([(j, r - 1) for j in range(r)], between=(r if r < IMAGES else None))
             if r < START_PAIRS:
                 run([(r, b) for b in range(r)])
-        sort_words(SORT_FROM)
         for j in range(START_PAIRS, PAIRS):
             if j + 1 < PAIRS:
                 transposes(j + 1)

@@ -118,10 +118,10 @@ def tile_spatialcgnl_pa_kernel(tc, x, Wt, Wp, Wg, out):
 
         def sort_words(j):
             for s in range(2):
-                wsort[(j, s)] = wsort_pool.tile([P, PASSES, 2, P], F32, name="wsort%d_%d" % (j, s), tag="wsort")
+                wsort[(j, s)] = wsort_pool.tile([P, 2, CIN // 4], F32, name="wsort%d_%d" % (j, s), tag="wsort")
                 nc.vector.tensor_copy(
-                    out=wsort[(j, s)][:],
-                    in_=wraw[j][s][:].bitcast(F32).rearrange("p (g c u) -> p g u c", g=PASSES, u=2),
+                    out=wsort[(j, s)][:].rearrange("p u (v f) -> p v u f", f=4),
+                    in_=wraw[j][s][:].bitcast(F32).rearrange("p (v f u) -> p v u f", f=4, u=2),
                 )
 
         def transposes(j):
@@ -136,7 +136,7 @@ def tile_spatialcgnl_pa_kernel(tc, x, Wt, Wp, Wg, out):
                         if j < SORT_FROM:
                             cols = words[:, 2 * P * g + u : 2 * P * g + 2 * P : 2]
                         else:
-                            cols = wsort[(j, s)][:, g, u, :]
+                            cols = wsort[(j, s)][:, u, P * g : P * g + P]
                         nc.tensor.transpose(tp[:, slot, :], cols, ident[:])
                     nc.scalar.copy(
                         out=regrouped[:].bitcast(F32)[:, BANK * half : BANK * half + BANK].rearrange(

@@ -27,6 +27,7 @@ PG_PAIRS = PANELS
 T_PAIRS = PANELS // 2
 PAIRS = PG_PAIRS + T_PAIRS
 START_PAIRS = IMAGES
+LAST_JOB = (PAIRS - 1, IMAGES - 1)
 SORT_FROM = START_PAIRS + 1
 
 FLOPS = 2 * 3 * CP * CIN * IMAGES * HW
@@ -81,6 +82,8 @@ def tile_spatialcgnl_pa_kernel(tc, x, Wt, Wp, Wg, out):
         make_identity(nc, ident[:])
         ones = const.tile([P, P], F32)
         nc.vector.memset(ones[:], 1.0)
+        zeros = const.tile([P, BANK], BF16, name="zeros")
+        nc.vector.memset(zeros[:], 0.0)
         part = const.tile([P, PG_PAIRS * IMAGES], F32)
         att = const.tile([P, GROUPS * IMAGES], F32)
         xc = [const.tile([P, PASSES * HW], U32, name="xc%d" % b, align_bytes=64) for b in range(IMAGES)]
@@ -124,8 +127,8 @@ def tile_spatialcgnl_pa_kernel(tc, x, Wt, Wp, Wg, out):
                     in_=wraw[j][s][:].bitcast(F32).rearrange("p (v f u) -> p v u f", f=4, u=2),
                 )
 
-        def transposes(j):
-            for s in range(2):
+        def transposes(j, panels=(0, 1)):
+            for s in panels:
                 words = wraw[j][s][:].bitcast(F32)
                 regrouped = wgrp_pool.tile([P, CIN], BF16, name="wgrp%d_%d" % (j, s), tag="wgrp", align_bytes=64)
                 wgrp[(j, s)] = regrouped
@@ -145,6 +148,13 @@ def tile_spatialcgnl_pa_kernel(tc, x, Wt, Wp, Wg, out):
                         in_=tp[:].rearrange("p (g u) m -> p g m u", g=2, u=2),
                     )
 
+        def warm_up(n):
+            idle = acc_pool.tile([P, 2, HW], F32, name="idle", tag="acc")
+            for i in range(n):
+                nc.tensor.matmul(
+                    idle[:].rearrange("p s n -> p (s n)"), lhsT=zeros[:, 0:P], rhs=zeros[:], start=True, stop=True
+                )
+
         def quantise_w(j):
             for s in range(2):
                 wc[(j, s)] = wq_pool.tile([P, PASSES * P], U32, name="wc%d_%d" % (j, s), tag="wc", align_bytes=64)
@@ -154,9 +164,10 @@ def tile_spatialcgnl_pa_kernel(tc, x, Wt, Wp, Wg, out):
                 )
 
         def job(j, b):
-            bank = acc_pool.tile([P, 2, HW], F32, name="acc%d_%d" % (j, b), tag="acc")
-            acc[(j, b)] = bank
             for s in range(2):
+                if s == 0 or (j, b) == LAST_JOB:
+                    bank = acc_pool.tile([P, 2, HW], F32, name="acc%d_%d_%d" % (j, b, s), tag="acc")
+                acc[(j, b, s)] = bank
                 for g in range(PASSES):
                     nc.tensor.matmul_mx(
                         out=bank[:, s, :],
@@ -169,7 +180,7 @@ def tile_spatialcgnl_pa_kernel(tc, x, Wt, Wp, Wg, out):
                     )
 
         def drain(j, b):
-            bank = acc[(j, b)]
+            bank = acc[(j, b, 0)]
             if j < PG_PAIRS:
                 p_sb = small.tile([P, HW], F32, name="p_sb%d_%d" % (j, b), tag="p_sb")
                 nc.scalar.copy(out=p_sb[:], in_=bank[:, 0, :])
@@ -187,12 +198,20 @@ def tile_spatialcgnl_pa_kernel(tc, x, Wt, Wp, Wg, out):
                 panel = 2 * (j - PG_PAIRS)
                 c, a = panel // PPG, panel % PPG
                 factor = att[:, c * IMAGES + b : c * IMAGES + b + 1]
+                dst = out[b, c].rearrange("(p a) n -> p a n", a=PPG)
+                if (j, b) == LAST_JOB:
+                    y_first = small.tile([P, HW], F32, name="y_first", tag="y_first")
+                    nc.vector.tensor_scalar(out=y_first[:], in0=bank[:, 0, :], scalar1=factor, scalar2=None, op0=MULT)
+                    nc.sync.dma_start(out=dst[:, a, :], in_=y_first[:])
+                    y_second = small.tile([P, HW], F32, name="y_second", tag="y_second")
+                    nc.scalar.activation(out=y_second[:], in_=acc[(j, b, 1)][:, 1, :], func=COPY, scale=factor)
+                    nc.sync.dma_start(out=dst[:, a + 1, :], in_=y_second[:])
+                    return
                 y_sb = small.tile([P, 2, HW], F32, name="y_sb%d_%d" % (j, b), tag="y_sb")
                 if b != 1:
                     nc.scalar.activation(out=y_sb[:], in_=bank[:], func=COPY, scale=factor)
                 else:
                     nc.vector.tensor_scalar(out=y_sb[:], in0=bank[:], scalar1=factor, scalar2=None, op0=MULT)
-                dst = out[b, c].rearrange("(p a) n -> p a n", a=PPG)
                 nc.sync.dma_start(out=dst[:, a : a + 2, :], in_=y_sb[:])
 
         def attention():
@@ -214,11 +233,18 @@ def tile_spatialcgnl_pa_kernel(tc, x, Wt, Wp, Wg, out):
             for j, b in jobs:
                 drain(j, b)
 
-        transposes(0)
+        warm_up(5)
+        transposes(0, panels=(0,))
+        warm_up(2)
+        transposes(0, panels=(1,))
         quantise_w(0)
+        warm_up(4)
         prep_x(0)
         for r in range(1, START_PAIRS + 1):
-            transposes(r)
+            transposes(r, panels=(0,))
+            if r == 1:
+                warm_up(2)
+            transposes(r, panels=(1,))
             quantise_w(r)
             if r >= SORT_FROM - 1:
                 sort_words(r + 1)

@@ -27,6 +27,11 @@ PG_PAIRS = PANELS
 T_PAIRS = PANELS // 2
 PAIRS = PG_PAIRS + T_PAIRS
 START_PAIRS = IMAGES
+BLOCK_PAIR = PAIRS - 1
+BLOCK_A = PPG - 2
+SQ = 32
+QUADS = P // SQ
+BLOCKS = PASSES * QUADS
 LAST_JOB = (PAIRS - 1, IMAGES - 1)
 SORT_FROM = START_PAIRS + 1
 
@@ -39,7 +44,10 @@ def tile_spatialcgnl_pa_kernel(tc, x, Wt, Wp, Wg, out):
         const = ctx.enter_context(tc.tile_pool(name="const", bufs=1))
         xraw_pool = ctx.enter_context(tc.tile_pool(name="xraw", bufs=IMAGES))
         xgrp_pool = ctx.enter_context(tc.tile_pool(name="xgrp", bufs=2))
-        wraw_pool = ctx.enter_context(tc.tile_pool(name="wraw", bufs=2 * PAIRS))
+        wraw_pool = ctx.enter_context(tc.tile_pool(name="wraw", bufs=18))
+        braw_pool = ctx.enter_context(tc.tile_pool(name="braw", bufs=1))
+        btr_pool = ctx.enter_context(tc.tile_pool(name="btr", bufs=1))
+        bgrp_pool = ctx.enter_context(tc.tile_pool(name="bgrp", bufs=2))
         wsort_pool = ctx.enter_context(tc.tile_pool(name="wsort", bufs=4))
         wgrp_pool = ctx.enter_context(tc.tile_pool(name="wgrp", bufs=4))
         wq_pool = ctx.enter_context(tc.tile_pool(name="wq", bufs=10))
@@ -59,8 +67,9 @@ def tile_spatialcgnl_pa_kernel(tc, x, Wt, Wp, Wg, out):
         xraw = [xraw_pool.tile([P, PASSES, PACK, HW], BF16, name="xraw%d" % b, tag="xraw") for b in range(IMAGES)]
         wraw = [
             [wraw_pool.tile([P, CIN], BF16, name="wraw%d_%d" % (j, s), tag="wraw") for s in range(2)]
-            for j in range(PAIRS)
+            for j in range(BLOCK_PAIR)
         ]
+        braw = braw_pool.tile([P, 2, PASSES, QUADS, 4 * SQ], BF16, name="braw")
 
         def load_x(b):
             src = x[b].rearrange("(g p t) h w -> p g (t h w)", g=PASSES, p=P, t=PACK)
@@ -73,17 +82,27 @@ def tile_spatialcgnl_pa_kernel(tc, x, Wt, Wp, Wg, out):
             for s in range(2):
                 nc.sync.dma_start(out=wraw[j][s][:], in_=panel_in_dram(j, s))
 
-        for j in range(PAIRS):
+        def load_blocks():
+            src = Wt.rearrange(
+                "(c r b a) (g i w) -> c r i b (a g) w", c=GROUPS, r=QUADS, b=SQ, a=PPG, g=PASSES, i=QUADS
+            )
+            for r in range(QUADS):
+                for i in (0, 2, 1, 3):
+                    nc.sync.dma_start(
+                        out=braw[SQ * i : SQ * i + SQ, :, :, r, :].rearrange("p s g w -> p (s g) w"),
+                        in_=src[GROUPS - 1, r, i][:, PASSES * BLOCK_A : PASSES * BLOCK_A + 2 * PASSES, :],
+                    )
+
+        for j in range(BLOCK_PAIR):
             load_w(j)
             if j < START_PAIRS:
                 load_x(j)
+        load_blocks()
 
         ident = const.tile([P, P], F32)
         make_identity(nc, ident[:])
         ones = const.tile([P, P], F32)
         nc.vector.memset(ones[:], 1.0)
-        zeros = const.tile([P, BANK], BF16, name="zeros")
-        nc.vector.memset(zeros[:], 0.0)
         part = const.tile([P, PG_PAIRS * IMAGES], F32)
         att = const.tile([P, GROUPS * IMAGES], F32)
         xc = [const.tile([P, PASSES * HW], U32, name="xc%d" % b, align_bytes=64) for b in range(IMAGES)]
@@ -93,6 +112,7 @@ def tile_spatialcgnl_pa_kernel(tc, x, Wt, Wp, Wg, out):
         ws = {}
         wsort = {}
         wgrp = {}
+        bturned = {}
         acc = {}
 
         def prep_x(b):
@@ -121,14 +141,14 @@ def tile_spatialcgnl_pa_kernel(tc, x, Wt, Wp, Wg, out):
 
         def sort_words(j):
             for s in range(2):
-                wsort[(j, s)] = wsort_pool.tile([P, 2, CIN // 4], F32, name="wsort%d_%d" % (j, s), tag="wsort")
+                wsort[(j, s)] = wsort_pool.tile([P, 2, CIN // 4], F32, name="wsort%d_%d" % (j, s), tag="wsort", align_bytes=64)
                 nc.vector.tensor_copy(
                     out=wsort[(j, s)][:].rearrange("p u (v f) -> p v u f", f=4),
                     in_=wraw[j][s][:].bitcast(F32).rearrange("p (v f u) -> p v u f", f=4, u=2),
                 )
 
-        def transposes(j, panels=(0, 1)):
-            for s in panels:
+        def transposes(j):
+            for s in range(2):
                 words = wraw[j][s][:].bitcast(F32)
                 regrouped = wgrp_pool.tile([P, CIN], BF16, name="wgrp%d_%d" % (j, s), tag="wgrp", align_bytes=64)
                 wgrp[(j, s)] = regrouped
@@ -148,12 +168,23 @@ def tile_spatialcgnl_pa_kernel(tc, x, Wt, Wp, Wg, out):
                         in_=tp[:].rearrange("p (g u) m -> p g m u", g=2, u=2),
                     )
 
-        def warm_up(n):
-            idle = acc_pool.tile([P, 2, HW], F32, name="idle", tag="acc")
-            for i in range(n):
-                nc.tensor.matmul(
-                    idle[:].rearrange("p s n -> p (s n)"), lhsT=zeros[:, 0:P], rhs=zeros[:], start=True, stop=True
-                )
+        def transpose_blocks(s):
+            ordered = wsort_pool.tile([P, BLOCKS, 2, SQ], F32, name="bsort%d" % s, tag="wsort", align_bytes=64)
+            nc.vector.tensor_copy(
+                out=ordered[:],
+                in_=braw[:, s].rearrange("p g r w -> p (g r w)").bitcast(F32).rearrange(
+                    "p (n q u) -> p n u q", n=BLOCKS, u=2
+                ),
+            )
+            bturned[s] = btr_pool.tile([P, BLOCKS * 2 * SQ], F32, name="btr%d" % s, tag="btr", align_bytes=64)
+            nc.vector.transpose(out=bturned[s][:], in_=ordered[:].rearrange("p n u q -> p (n u q)"))
+
+        def regroup_blocks(s):
+            wgrp[(BLOCK_PAIR, s)] = bgrp_pool.tile([P, CIN], BF16, name="bgrp%d" % s, tag="bgrp", align_bytes=64)
+            nc.scalar.copy(
+                out=wgrp[(BLOCK_PAIR, s)][:].bitcast(F32).rearrange("p (n b u) -> p n b u", n=BLOCKS, u=2),
+                in_=bturned[s][:].rearrange("p (n u b) -> p n b u", n=BLOCKS, u=2),
+            )
 
         def quantise_w(j):
             for s in range(2):
@@ -233,18 +264,11 @@ def tile_spatialcgnl_pa_kernel(tc, x, Wt, Wp, Wg, out):
             for j, b in jobs:
                 drain(j, b)
 
-        warm_up(5)
-        transposes(0, panels=(0,))
-        warm_up(2)
-        transposes(0, panels=(1,))
+        transposes(0)
         quantise_w(0)
-        warm_up(4)
         prep_x(0)
         for r in range(1, START_PAIRS + 1):
-            transposes(r, panels=(0,))
-            if r == 1:
-                warm_up(2)
-            transposes(r, panels=(1,))
+            transposes(r)
             quantise_w(r)
             if r >= SORT_FROM - 1:
                 sort_words(r + 1)
@@ -252,12 +276,18 @@ def tile_spatialcgnl_pa_kernel(tc, x, Wt, Wp, Wg, out):
             if r < START_PAIRS:
                 run([(r, b) for b in range(r)])
         for j in range(START_PAIRS, PAIRS):
-            if j + 1 < PAIRS:
+            if j + 1 < BLOCK_PAIR:
                 transposes(j + 1)
-                if j == PG_PAIRS:
-                    attention()
-                if j + 2 < PAIRS:
-                    sort_words(j + 2)
+            if BLOCK_PAIR - 2 <= j < BLOCK_PAIR:
+                regroup_blocks(j - (BLOCK_PAIR - 2))
+            if j + 2 < BLOCK_PAIR:
+                sort_words(j + 2)
+            if j + 1 < PAIRS:
                 quantise_w(j + 1)
             for b in range(IMAGES):
-                run([(j, b)])
+                job(j, b)
+                if (j, b) == (PG_PAIRS, 0):
+                    attention()
+                drain(j, b)
+                if b == 0 and BLOCK_PAIR - 3 <= j < BLOCK_PAIR - 1:
+                    transpose_blocks(j - (BLOCK_PAIR - 3))

@@ -27,8 +27,8 @@ PG_PAIRS = PANELS
 T_PAIRS = PANELS // 2
 PAIRS = PG_PAIRS + T_PAIRS
 START_PAIRS = IMAGES
-BLOCK_PAIR = PAIRS - 1
-BLOCK_A = PPG - 2
+FIRST_BLOCK_PAIR = PAIRS - T_PAIRS // GROUPS
+FIRST_TURN = FIRST_BLOCK_PAIR - PPG
 SQ = 32
 QUADS = P // SQ
 BLOCKS = PASSES * QUADS
@@ -44,9 +44,10 @@ def tile_spatialcgnl_pa_kernel(tc, x, Wt, Wp, Wg, out):
         const = ctx.enter_context(tc.tile_pool(name="const", bufs=1))
         xraw_pool = ctx.enter_context(tc.tile_pool(name="xraw", bufs=IMAGES))
         xgrp_pool = ctx.enter_context(tc.tile_pool(name="xgrp", bufs=2))
-        wraw_pool = ctx.enter_context(tc.tile_pool(name="wraw", bufs=18))
+        wraw_pool = ctx.enter_context(tc.tile_pool(name="wraw", bufs=14))
         braw_pool = ctx.enter_context(tc.tile_pool(name="braw", bufs=1))
-        btr_pool = ctx.enter_context(tc.tile_pool(name="btr", bufs=1))
+        bsort_pool = ctx.enter_context(tc.tile_pool(name="bsort", bufs=2))
+        btr_pool = ctx.enter_context(tc.tile_pool(name="btr", bufs=2))
         bgrp_pool = ctx.enter_context(tc.tile_pool(name="bgrp", bufs=2))
         wsort_pool = ctx.enter_context(tc.tile_pool(name="wsort", bufs=4))
         wgrp_pool = ctx.enter_context(tc.tile_pool(name="wgrp", bufs=4))
@@ -67,9 +68,9 @@ def tile_spatialcgnl_pa_kernel(tc, x, Wt, Wp, Wg, out):
         xraw = [xraw_pool.tile([P, PASSES, PACK, HW], BF16, name="xraw%d" % b, tag="xraw") for b in range(IMAGES)]
         wraw = [
             [wraw_pool.tile([P, CIN], BF16, name="wraw%d_%d" % (j, s), tag="wraw") for s in range(2)]
-            for j in range(BLOCK_PAIR)
+            for j in range(FIRST_BLOCK_PAIR)
         ]
-        braw = braw_pool.tile([P, 2, PASSES, QUADS, 4 * SQ], BF16, name="braw")
+        braw = braw_pool.tile([P, PPG, PASSES, QUADS, 4 * SQ], BF16, name="braw")
 
         def load_x(b):
             src = x[b].rearrange("(g p t) h w -> p g (t h w)", g=PASSES, p=P, t=PACK)
@@ -82,22 +83,23 @@ def tile_spatialcgnl_pa_kernel(tc, x, Wt, Wp, Wg, out):
             for s in range(2):
                 nc.sync.dma_start(out=wraw[j][s][:], in_=panel_in_dram(j, s))
 
-        def load_blocks():
+        def load_blocks(first):
             src = Wt.rearrange(
                 "(c r b a) (g i w) -> c r i b (a g) w", c=GROUPS, r=QUADS, b=SQ, a=PPG, g=PASSES, i=QUADS
             )
             for r in range(QUADS):
                 for i in (0, 2, 1, 3):
                     nc.sync.dma_start(
-                        out=braw[SQ * i : SQ * i + SQ, :, :, r, :].rearrange("p s g w -> p (s g) w"),
-                        in_=src[GROUPS - 1, r, i][:, PASSES * BLOCK_A : PASSES * BLOCK_A + 2 * PASSES, :],
+                        out=braw[SQ * i : SQ * i + SQ, first : first + 2, :, r, :].rearrange("p a g w -> p (a g) w"),
+                        in_=src[GROUPS - 1, r, i][:, PASSES * first : PASSES * first + 2 * PASSES, :],
                     )
 
-        for j in range(BLOCK_PAIR):
+        for j in range(FIRST_BLOCK_PAIR):
             load_w(j)
             if j < START_PAIRS:
                 load_x(j)
-        load_blocks()
+        for first in range(0, PPG, 2):
+            load_blocks(first)
 
         ident = const.tile([P, P], F32)
         make_identity(nc, ident[:])
@@ -112,6 +114,7 @@ def tile_spatialcgnl_pa_kernel(tc, x, Wt, Wp, Wg, out):
         ws = {}
         wsort = {}
         wgrp = {}
+        bsort = {}
         bturned = {}
         acc = {}
 
@@ -168,22 +171,22 @@ def tile_spatialcgnl_pa_kernel(tc, x, Wt, Wp, Wg, out):
                         in_=tp[:].rearrange("p (g u) m -> p g m u", g=2, u=2),
                     )
 
-        def transpose_blocks(s):
-            ordered = wsort_pool.tile([P, BLOCKS, 2, SQ], F32, name="bsort%d" % s, tag="wsort", align_bytes=64)
-            nc.vector.tensor_copy(
-                out=ordered[:],
-                in_=braw[:, s].rearrange("p g r w -> p (g r w)").bitcast(F32).rearrange(
-                    "p (n q u) -> p n u q", n=BLOCKS, u=2
-                ),
-            )
-            bturned[s] = btr_pool.tile([P, BLOCKS * 2 * SQ], F32, name="btr%d" % s, tag="btr", align_bytes=64)
-            nc.vector.transpose(out=bturned[s][:], in_=ordered[:].rearrange("p n u q -> p (n u q)"))
 
-        def regroup_blocks(s):
-            wgrp[(BLOCK_PAIR, s)] = bgrp_pool.tile([P, CIN], BF16, name="bgrp%d" % s, tag="bgrp", align_bytes=64)
+        def sort_blocks(engine_copy, a):
+            bsort[a] = bsort_pool.tile([P, BLOCKS, 2, SQ], F32, name="bsort%d" % a, tag="bsort", align_bytes=64)
+            words = braw[:, a].rearrange("p g r w -> p (g r w)").bitcast(F32)
+            engine_copy(out=bsort[a][:], in_=words.rearrange("p (n q u) -> p n u q", n=BLOCKS, u=2))
+
+        def transpose_blocks(a):
+            bturned[a] = btr_pool.tile([P, BLOCKS * 2 * SQ], F32, name="btr%d" % a, tag="btr", align_bytes=64)
+            nc.vector.transpose(out=bturned[a][:], in_=bsort[a][:].rearrange("p n u q -> p (n u q)"))
+
+        def regroup_blocks(a):
+            regrouped = bgrp_pool.tile([P, CIN], BF16, name="bgrp%d" % a, tag="bgrp", align_bytes=64)
+            wgrp[(FIRST_BLOCK_PAIR + a // 2, a % 2)] = regrouped
             nc.scalar.copy(
-                out=wgrp[(BLOCK_PAIR, s)][:].bitcast(F32).rearrange("p (n b u) -> p n b u", n=BLOCKS, u=2),
-                in_=bturned[s][:].rearrange("p (n u b) -> p n b u", n=BLOCKS, u=2),
+                out=regrouped[:].bitcast(F32).rearrange("p (n b u) -> p n b u", n=BLOCKS, u=2),
+                in_=bturned[a][:].rearrange("p (n u b) -> p n b u", n=BLOCKS, u=2),
             )
 
         def quantise_w(j):
@@ -231,14 +234,14 @@ def tile_spatialcgnl_pa_kernel(tc, x, Wt, Wp, Wg, out):
                 factor = att[:, c * IMAGES + b : c * IMAGES + b + 1]
                 dst = out[b, c].rearrange("(p a) n -> p a n", a=PPG)
                 if (j, b) == LAST_JOB:
-                    y_first = small.tile([P, HW], F32, name="y_first", tag="y_first")
+                    y_first = small.tile([P, HW], F32, name="y_first", tag="y_first", bufs=1)
                     nc.vector.tensor_scalar(out=y_first[:], in0=bank[:, 0, :], scalar1=factor, scalar2=None, op0=MULT)
                     nc.sync.dma_start(out=dst[:, a, :], in_=y_first[:])
-                    y_second = small.tile([P, HW], F32, name="y_second", tag="y_second")
+                    y_second = small.tile([P, HW], F32, name="y_second", tag="y_second", bufs=1)
                     nc.scalar.activation(out=y_second[:], in_=acc[(j, b, 1)][:, 1, :], func=COPY, scale=factor)
                     nc.sync.dma_start(out=dst[:, a + 1, :], in_=y_second[:])
                     return
-                y_sb = small.tile([P, 2, HW], F32, name="y_sb%d_%d" % (j, b), tag="y_sb")
+                y_sb = small.tile([P, 2, HW], F32, name="y_sb%d_%d" % (j, b), tag="y_sb", bufs=6)
                 if b != 1:
                     nc.scalar.activation(out=y_sb[:], in_=bank[:], func=COPY, scale=factor)
                 else:
@@ -276,18 +279,29 @@ def tile_spatialcgnl_pa_kernel(tc, x, Wt, Wp, Wg, out):
             if r < START_PAIRS:
                 run([(r, b) for b in range(r)])
         for j in range(START_PAIRS, PAIRS):
-            if j + 1 < BLOCK_PAIR:
+            turn = j - FIRST_TURN
+            if j + 1 < FIRST_BLOCK_PAIR:
                 transposes(j + 1)
-            if BLOCK_PAIR - 2 <= j < BLOCK_PAIR:
-                regroup_blocks(j - (BLOCK_PAIR - 2))
-            if j + 2 < BLOCK_PAIR:
+            if 0 <= turn < PPG and j < PG_PAIRS:
+                sort_blocks(nc.scalar.copy, turn)
+            if j == FIRST_BLOCK_PAIR - 2:
+                regroup_blocks(0)
+            if j == FIRST_BLOCK_PAIR - 1:
+                regroup_blocks(1)
+            if j == FIRST_BLOCK_PAIR:
+                regroup_blocks(3)
+            if j + 2 < FIRST_BLOCK_PAIR:
                 sort_words(j + 2)
             if j + 1 < PAIRS:
                 quantise_w(j + 1)
+            if j == FIRST_BLOCK_PAIR - 1:
+                regroup_blocks(2)
             for b in range(IMAGES):
                 job(j, b)
                 if (j, b) == (PG_PAIRS, 0):
                     attention()
                 drain(j, b)
-                if b == 0 and BLOCK_PAIR - 3 <= j < BLOCK_PAIR - 1:
-                    transpose_blocks(j - (BLOCK_PAIR - 3))
+                if b == 0 and 0 <= turn < PPG:
+                    if j >= PG_PAIRS:
+                        sort_blocks(nc.vector.tensor_copy, turn)
+                    transpose_blocks(turn)

@@ -146,8 +146,8 @@ def tile_spatialcgnl_pa_kernel(tc, x, Wt, Wp, Wg, out):
             for s in range(2):
                 wsort[(j, s)] = wsort_pool.tile([P, 2, CIN // 4], F32, name="wsort%d_%d" % (j, s), tag="wsort", align_bytes=64)
                 nc.vector.tensor_copy(
-                    out=wsort[(j, s)][:].rearrange("p u (v f) -> p v u f", f=4),
-                    in_=wraw[j][s][:].bitcast(F32).rearrange("p (v f u) -> p v u f", f=4, u=2),
+                    out=wsort[(j, s)][:].rearrange("p u n -> p n u"),
+                    in_=wraw[j][s][:].bitcast(F32).rearrange("p (n u) -> p n u", u=2),
                 )
 
         def transposes(j):
@@ -175,7 +175,7 @@ def tile_spatialcgnl_pa_kernel(tc, x, Wt, Wp, Wg, out):
         def sort_blocks(engine_copy, a):
             bsort[a] = bsort_pool.tile([P, BLOCKS, 2, SQ], F32, name="bsort%d" % a, tag="bsort", align_bytes=64)
             words = braw[:, a].rearrange("p g r w -> p (g r w)").bitcast(F32)
-            engine_copy(out=bsort[a][:], in_=words.rearrange("p (n q u) -> p n u q", n=BLOCKS, u=2))
+            engine_copy(out=bsort[a][:].rearrange("p n u q -> p n q u"), in_=words.rearrange("p (n q u) -> p n q u", n=BLOCKS, u=2))
 
         def transpose_blocks(a):
             bturned[a] = btr_pool.tile([P, BLOCKS * 2 * SQ], F32, name="btr%d" % a, tag="btr", align_bytes=64)

@@ -27,8 +27,9 @@ PG_PAIRS = PANELS
 T_PAIRS = PANELS // 2
 PAIRS = PG_PAIRS + T_PAIRS
 START_PAIRS = IMAGES
-FIRST_BLOCK_PAIR = PAIRS - T_PAIRS // GROUPS
-FIRST_TURN = FIRST_BLOCK_PAIR - PPG
+FIRST_BLOCK_PAIR = PAIRS - 3
+BLOCK_PANELS = 2 * (PAIRS - FIRST_BLOCK_PAIR)
+FIRST_TURN = START_PAIRS + 1
 SQ = 32
 QUADS = P // SQ
 BLOCKS = PASSES * QUADS
@@ -44,11 +45,11 @@ def tile_spatialcgnl_pa_kernel(tc, x, Wt, Wp, Wg, out):
         const = ctx.enter_context(tc.tile_pool(name="const", bufs=1))
         xraw_pool = ctx.enter_context(tc.tile_pool(name="xraw", bufs=IMAGES))
         xgrp_pool = ctx.enter_context(tc.tile_pool(name="xgrp", bufs=2))
-        wraw_pool = ctx.enter_context(tc.tile_pool(name="wraw", bufs=14))
+        wraw_pool = ctx.enter_context(tc.tile_pool(name="wraw", bufs=10))
         braw_pool = ctx.enter_context(tc.tile_pool(name="braw", bufs=1))
         bsort_pool = ctx.enter_context(tc.tile_pool(name="bsort", bufs=2))
         btr_pool = ctx.enter_context(tc.tile_pool(name="btr", bufs=2))
-        bgrp_pool = ctx.enter_context(tc.tile_pool(name="bgrp", bufs=2))
+        bgrp_pool = ctx.enter_context(tc.tile_pool(name="bgrp", bufs=4))
         wsort_pool = ctx.enter_context(tc.tile_pool(name="wsort", bufs=4))
         wgrp_pool = ctx.enter_context(tc.tile_pool(name="wgrp", bufs=4))
         wq_pool = ctx.enter_context(tc.tile_pool(name="wq", bufs=10))
@@ -70,7 +71,7 @@ def tile_spatialcgnl_pa_kernel(tc, x, Wt, Wp, Wg, out):
             [wraw_pool.tile([P, CIN], BF16, name="wraw%d_%d" % (j, s), tag="wraw") for s in range(2)]
             for j in range(FIRST_BLOCK_PAIR)
         ]
-        braw = braw_pool.tile([P, PPG, PASSES, QUADS, 4 * SQ], BF16, name="braw")
+        braw = braw_pool.tile([P, BLOCK_PANELS, PASSES, QUADS, 4 * SQ], BF16, name="braw")
 
         def load_x(b):
             src = x[b].rearrange("(g p t) h w -> p g (t h w)", g=PASSES, p=P, t=PACK)
@@ -83,7 +84,9 @@ def tile_spatialcgnl_pa_kernel(tc, x, Wt, Wp, Wg, out):
             for s in range(2):
                 nc.sync.dma_start(out=wraw[j][s][:], in_=panel_in_dram(j, s))
 
-        def load_blocks(first):
+        def load_blocks(j):
+            first = 2 * (j - FIRST_BLOCK_PAIR)
+            c, a = (j - PG_PAIRS) * 2 // PPG, (j - PG_PAIRS) * 2 % PPG
             src = Wt.rearrange(
                 "(c r b a) (g i w) -> c r i b (a g) w", c=GROUPS, r=QUADS, b=SQ, a=PPG, g=PASSES, i=QUADS
             )
@@ -91,15 +94,17 @@ def tile_spatialcgnl_pa_kernel(tc, x, Wt, Wp, Wg, out):
                 for i in (0, 2, 1, 3):
                     nc.sync.dma_start(
                         out=braw[SQ * i : SQ * i + SQ, first : first + 2, :, r, :].rearrange("p a g w -> p (a g) w"),
-                        in_=src[GROUPS - 1, r, i][:, PASSES * first : PASSES * first + 2 * PASSES, :],
+                        in_=src[c, r, i][:, PASSES * a : PASSES * a + 2 * PASSES, :],
                     )
 
         for j in range(FIRST_BLOCK_PAIR):
+            if j == FIRST_TURN + 3:
+                load_blocks(FIRST_BLOCK_PAIR)
             load_w(j)
             if j < START_PAIRS:
                 load_x(j)
-        for first in range(0, PPG, 2):
-            load_blocks(first)
+        for j in range(FIRST_BLOCK_PAIR + 1, PAIRS):
+            load_blocks(j)
 
         ident = const.tile([P, P], F32)
         make_identity(nc, ident[:])
@@ -107,8 +112,8 @@ def tile_spatialcgnl_pa_kernel(tc, x, Wt, Wp, Wg, out):
         nc.vector.memset(ones[:], 1.0)
         part = const.tile([P, PG_PAIRS * IMAGES], F32)
         att = const.tile([P, GROUPS * IMAGES], F32)
-        xc = [const.tile([P, PASSES * HW], U32, name="xc%d" % b, align_bytes=64) for b in range(IMAGES)]
-        xs = [const.tile([P, PASSES * HW], U8, name="xs%d" % b, align_bytes=64) for b in range(IMAGES)]
+        xc = [const.tile([P, PASSES * HW], U32, name="xc%d" % b, align_bytes=256) for b in range(IMAGES)]
+        xs = [const.tile([P, PASSES * HW], U8, name="xs%d" % b, align_bytes=256) for b in range(IMAGES)]
 
         wc = {}
         ws = {}
@@ -172,27 +177,45 @@ def tile_spatialcgnl_pa_kernel(tc, x, Wt, Wp, Wg, out):
                     )
 
 
-        def sort_blocks(engine_copy, a):
-            bsort[a] = bsort_pool.tile([P, BLOCKS, 2, SQ], F32, name="bsort%d" % a, tag="bsort", align_bytes=64)
-            words = braw[:, a].rearrange("p g r w -> p (g r w)").bitcast(F32)
-            engine_copy(out=bsort[a][:].rearrange("p n u q -> p n q u"), in_=words.rearrange("p (n q u) -> p n q u", n=BLOCKS, u=2))
+        def sort_blocks(engine_copy, k):
+            bsort[k] = bsort_pool.tile([P, BLOCKS, 2, SQ], F32, name="bsort%d" % k, tag="bsort", align_bytes=64)
+            words = braw[:, k].rearrange("p g r w -> p (g r w)").bitcast(F32)
+            engine_copy(out=bsort[k][:].rearrange("p n u q -> p n q u"), in_=words.rearrange("p (n q u) -> p n q u", n=BLOCKS, u=2))
 
-        def transpose_blocks(a):
-            bturned[a] = btr_pool.tile([P, BLOCKS * 2 * SQ], F32, name="btr%d" % a, tag="btr", align_bytes=64)
-            nc.vector.transpose(out=bturned[a][:], in_=bsort[a][:].rearrange("p n u q -> p (n u q)"))
+        def transpose_blocks(k):
+            bturned[k] = btr_pool.tile([P, BLOCKS * 2 * SQ], F32, name="btr%d" % k, tag="btr", align_bytes=64)
+            nc.vector.transpose(out=bturned[k][:], in_=bsort[k][:].rearrange("p n u q -> p (n u q)"))
 
-        def regroup_blocks(a):
-            regrouped = bgrp_pool.tile([P, CIN], BF16, name="bgrp%d" % a, tag="bgrp", align_bytes=64)
-            wgrp[(FIRST_BLOCK_PAIR + a // 2, a % 2)] = regrouped
+        def regroup_blocks(k):
+            regrouped = bgrp_pool.tile([P, CIN], BF16, name="bgrp%d" % k, tag="bgrp", align_bytes=64)
+            wgrp[(FIRST_BLOCK_PAIR + k // 2, k % 2)] = regrouped
             nc.scalar.copy(
                 out=regrouped[:].bitcast(F32).rearrange("p (n b u) -> p n b u", n=BLOCKS, u=2),
-                in_=bturned[a][:].rearrange("p (n u b) -> p n b u", n=BLOCKS, u=2),
+                in_=bturned[k][:].rearrange("p (n u b) -> p n b u", n=BLOCKS, u=2),
             )
+
+        def block_step(j, b):
+            turn = j - FIRST_TURN
+            if not 0 <= turn < BLOCK_PANELS:
+                return
+            k = turn // 2 * 2
+            if turn % 2 == 0:
+                if b == 0:
+                    sort_blocks(nc.vector.tensor_copy if j < PG_PAIRS else nc.scalar.copy, k)
+                if b == 1:
+                    sort_blocks(nc.scalar.copy, k + 1)
+                    transpose_blocks(k)
+            else:
+                if b == 0:
+                    transpose_blocks(k + 1)
+                    regroup_blocks(k)
+                if b == 2:
+                    regroup_blocks(k + 1)
 
         def quantise_w(j):
             for s in range(2):
-                wc[(j, s)] = wq_pool.tile([P, PASSES * P], U32, name="wc%d_%d" % (j, s), tag="wc", align_bytes=64)
-                ws[(j, s)] = wq_pool.tile([P, PASSES * P], U8, name="ws%d_%d" % (j, s), tag="ws", align_bytes=64)
+                wc[(j, s)] = wq_pool.tile([P, PASSES * P], U32, name="wc%d_%d" % (j, s), tag="wc", align_bytes=256)
+                ws[(j, s)] = wq_pool.tile([P, PASSES * P], U8, name="ws%d_%d" % (j, s), tag="ws", align_bytes=256)
                 nc.vector.quantize_mx(
                     out=wc[(j, s)][:].bitcast(FP8X4), scales=ws[(j, s)][:], in_=wgrp[(j, s)][:]
                 )
@@ -248,16 +271,25 @@ def tile_spatialcgnl_pa_kernel(tc, x, Wt, Wp, Wg, out):
                     nc.vector.tensor_scalar(out=y_sb[:], in0=bank[:], scalar1=factor, scalar2=None, op0=MULT)
                 nc.sync.dma_start(out=dst[:, a : a + 2, :], in_=y_sb[:])
 
-        def attention():
-            att_ps = tp_pool.tile([P, 4, P], F32, name="att_ps", tag="tp")
-            sums = att_ps[:, 0, 0 : PG_PAIRS * IMAGES]
-            nc.tensor.matmul(sums, lhsT=ones[:], rhs=part[:], start=True, stop=True)
+        def attention(c):
+            n = PPG * IMAGES
+            att_ps = tp_pool.tile([P, 4, P], F32, name="att_ps%d" % c, tag="tp")
+            sums = att_ps[:, 0, 0:n]
+            nc.tensor.matmul(sums, lhsT=ones[:], rhs=part[:, n * c : n * c + n], start=True, stop=True)
             nc.vector.tensor_reduce(
-                out=att[:].rearrange("p (c b) -> p c b", c=GROUPS),
-                in_=sums.rearrange("p (c a b) -> p c b a", c=GROUPS, a=PPG, b=IMAGES),
+                out=att[:, IMAGES * c : IMAGES * c + IMAGES],
+                in_=sums.rearrange("p (a b) -> p b a", a=PPG, b=IMAGES),
                 axis=mybir.AxisListType.X,
                 op=ADD,
             )
+
+        def run(jobs, between=None):
+            for j, b in jobs:
+                job(j, b)
+            if between is not None:
+                prep_x(between)
+            for j, b in jobs:
+                drain(j, b)
 
         def run(jobs, between=None):
             for j, b in jobs:
@@ -279,29 +311,15 @@ def tile_spatialcgnl_pa_kernel(tc, x, Wt, Wp, Wg, out):
             if r < START_PAIRS:
                 run([(r, b) for b in range(r)])
         for j in range(START_PAIRS, PAIRS):
-            turn = j - FIRST_TURN
             if j + 1 < FIRST_BLOCK_PAIR:
                 transposes(j + 1)
-            if 0 <= turn < PPG and j < PG_PAIRS:
-                sort_blocks(nc.scalar.copy, turn)
-            if j == FIRST_BLOCK_PAIR - 2:
-                regroup_blocks(0)
-            if j == FIRST_BLOCK_PAIR - 1:
-                regroup_blocks(1)
-            if j == FIRST_BLOCK_PAIR:
-                regroup_blocks(3)
             if j + 2 < FIRST_BLOCK_PAIR:
                 sort_words(j + 2)
+            if j >= PG_PAIRS and (j - PG_PAIRS) * 2 % PPG == 0:
+                attention((j - PG_PAIRS) * 2 // PPG)
             if j + 1 < PAIRS:
                 quantise_w(j + 1)
-            if j == FIRST_BLOCK_PAIR - 1:
-                regroup_blocks(2)
             for b in range(IMAGES):
                 job(j, b)
-                if (j, b) == (PG_PAIRS, 0):
-                    attention()
                 drain(j, b)
-                if b == 0 and 0 <= turn < PPG:
-                    if j >= PG_PAIRS:
-                        sort_blocks(nc.vector.tensor_copy, turn)
-                    transpose_blocks(turn)
+                block_step(j, b)

from contextlib import ExitStack

import concourse.mybir as mybir
from concourse.masks import make_identity

F32 = mybir.dt.float32
BF16 = mybir.dt.bfloat16
U32 = mybir.dt.uint32
U8 = mybir.dt.uint8
FP8X4 = mybir.dt.float8_e4m3fn_x4
MULT = mybir.AluOpType.mult
ADD = mybir.AluOpType.add
COPY = mybir.ActivationFunctionType.Copy

P = 128
PACK = 4
BANK = 512
IMAGES = 3
CIN = 2048
HW = 256
CP = 1024
GROUPS = 2
PASSES = CIN // (P * PACK)
PANELS = CP // P
PPG = PANELS // GROUPS
PG_PAIRS = PANELS
T_PAIRS = PANELS // 2
PAIRS = PG_PAIRS + T_PAIRS
START_PAIRS = IMAGES
FIRST_BLOCK_PAIR = PAIRS - 3
BLOCK_PANELS = 2 * (PAIRS - FIRST_BLOCK_PAIR)
FIRST_TURN = START_PAIRS + 1
SQ = 32
QUADS = P // SQ
BLOCKS = PASSES * QUADS
LAST_JOB = (PAIRS - 1, IMAGES - 1)
SORT_FROM = START_PAIRS + 1

FLOPS = 2 * 3 * CP * CIN * IMAGES * HW


def tile_spatialcgnl_pa_kernel(tc, x, Wt, Wp, Wg, out):
    nc = tc.nc
    with ExitStack() as ctx:
        const = ctx.enter_context(tc.tile_pool(name="const", bufs=1))
        xraw_pool = ctx.enter_context(tc.tile_pool(name="xraw", bufs=IMAGES))
        xgrp_pool = ctx.enter_context(tc.tile_pool(name="xgrp", bufs=2))
        wraw_pool = ctx.enter_context(tc.tile_pool(name="wraw", bufs=10))
        braw_pool = ctx.enter_context(tc.tile_pool(name="braw", bufs=1))
        bsort_pool = ctx.enter_context(tc.tile_pool(name="bsort", bufs=2))
        btr_pool = ctx.enter_context(tc.tile_pool(name="btr", bufs=2))
        bgrp_pool = ctx.enter_context(tc.tile_pool(name="bgrp", bufs=4))
        wsort_pool = ctx.enter_context(tc.tile_pool(name="wsort", bufs=4))
        wgrp_pool = ctx.enter_context(tc.tile_pool(name="wgrp", bufs=4))
        wq_pool = ctx.enter_context(tc.tile_pool(name="wq", bufs=10))
        small = ctx.enter_context(tc.tile_pool(name="small", bufs=4))
        tp_pool = ctx.enter_context(tc.psum_pool(name="tp", bufs=4))
        acc_pool = ctx.enter_context(tc.psum_pool(name="acc", bufs=4))
        ctx.enter_context(tc.manual_schedule())

        def panel_in_dram(j, s):
            if j < PG_PAIRS:
                w, panel = (Wp, Wg)[s], j
            else:
                w, panel = Wt, 2 * (j - PG_PAIRS) + s
            view = w.rearrange("(c p a) k -> c a p k", c=GROUPS, p=P, a=PPG)
            return view[panel // PPG, panel % PPG]

        xraw = [xraw_pool.tile([P, PASSES, PACK, HW], BF16, name="xraw%d" % b, tag="xraw") for b in range(IMAGES)]
        wraw = [
            [wraw_pool.tile([P, CIN], BF16, name="wraw%d_%d" % (j, s), tag="wraw") for s in range(2)]
            for j in range(FIRST_BLOCK_PAIR)
        ]
        braw = braw_pool.tile([P, BLOCK_PANELS, PASSES, QUADS, 4 * SQ], BF16, name="braw")

        def load_x(b):
            src = x[b].rearrange("(g p t) h w -> p g (t h w)", g=PASSES, p=P, t=PACK)
            dst = xraw[b][:].rearrange("p g t n -> p g (t n)")
            for half in range(2):
                chunks = slice(2 * half, 2 * half + 2)
                nc.sync.dma_start(out=dst[:, chunks, :], in_=src[:, chunks, :])

        def load_w(j):
            for s in range(2):
                nc.sync.dma_start(out=wraw[j][s][:], in_=panel_in_dram(j, s))

        def load_blocks(j):
            first = 2 * (j - FIRST_BLOCK_PAIR)
            c, a = (j - PG_PAIRS) * 2 // PPG, (j - PG_PAIRS) * 2 % PPG
            src = Wt.rearrange(
                "(c r b a) (g i w) -> c r i b (a g) w", c=GROUPS, r=QUADS, b=SQ, a=PPG, g=PASSES, i=QUADS
            )
            for r in range(QUADS):
                for i in (0, 2, 1, 3):
                    nc.sync.dma_start(
                        out=braw[SQ * i : SQ * i + SQ, first : first + 2, :, r, :].rearrange("p a g w -> p (a g) w"),
                        in_=src[c, r, i][:, PASSES * a : PASSES * a + 2 * PASSES, :],
                    )

        for j in range(FIRST_BLOCK_PAIR):
            if j == FIRST_TURN + 3:
                load_blocks(FIRST_BLOCK_PAIR)
            load_w(j)
            if j < START_PAIRS:
                load_x(j)
        for j in range(FIRST_BLOCK_PAIR + 1, PAIRS):
            load_blocks(j)

        ident = const.tile([P, P], F32)
        make_identity(nc, ident[:])
        ones = const.tile([P, P], F32)
        nc.vector.memset(ones[:], 1.0)
        part = const.tile([P, PG_PAIRS * IMAGES], F32)
        att = const.tile([P, GROUPS * IMAGES], F32)
        xc = [const.tile([P, PASSES * HW], U32, name="xc%d" % b, align_bytes=256) for b in range(IMAGES)]
        xs = [const.tile([P, PASSES * HW], U8, name="xs%d" % b, align_bytes=256) for b in range(IMAGES)]

        wc = {}
        ws = {}
        wsort = {}
        wgrp = {}
        bsort = {}
        bturned = {}
        acc = {}

        def prep_x(b):
            xgrp = xgrp_pool.tile([P, PASSES, HW, PACK], BF16, name="xgrp%d" % b, tag="xgrp", align_bytes=64)

            def regroup(engine_copy, g):
                engine_copy(
                    out=xgrp[:, g].rearrange("p (v f) t -> p v t f", f=4),
                    in_=xraw[b][:, g].rearrange("p t (v f) -> p v t f", f=4),
                )

            def quantise(half):
                cols = slice(2 * HW * half, 2 * HW * half + 2 * HW)
                nc.vector.quantize_mx(
                    out=xc[b][:, cols].bitcast(FP8X4),
                    scales=xs[b][:, cols],
                    in_=xgrp[:, 2 * half : 2 * half + 2].rearrange("p g n t -> p (g n t)"),
                )

            regroup(nc.vector.tensor_copy, 0)
            regroup(nc.vector.tensor_copy, 1)
            regroup(nc.scalar.copy, 3)
            regroup(nc.vector.tensor_copy, 2)
            quantise(0)
            quantise(1)

        def sort_words(j):
            for s in range(2):
                wsort[(j, s)] = wsort_pool.tile([P, 2, CIN // 4], F32, name="wsort%d_%d" % (j, s), tag="wsort", align_bytes=64)
                nc.vector.tensor_copy(
                    out=wsort[(j, s)][:].rearrange("p u n -> p n u"),
                    in_=wraw[j][s][:].bitcast(F32).rearrange("p (n u) -> p n u", u=2),
                )

        def transposes(j):
            for s in range(2):
                words = wraw[j][s][:].bitcast(F32)
                regrouped = wgrp_pool.tile([P, CIN], BF16, name="wgrp%d_%d" % (j, s), tag="wgrp", align_bytes=64)
                wgrp[(j, s)] = regrouped
                for half in range(2):
                    tp = tp_pool.tile([P, 4, P], F32, name="tp%d_%d_%d" % (j, s, half), tag="tp")
                    for slot in range(4):
                        g, u = 2 * half + slot // 2, slot % 2
                        if j < SORT_FROM:
                            cols = words[:, 2 * P * g + u : 2 * P * g + 2 * P : 2]
                        else:
                            cols = wsort[(j, s)][:, u, P * g : P * g + P]
                        nc.tensor.transpose(tp[:, slot, :], cols, ident[:])
                    nc.scalar.copy(
                        out=regrouped[:].bitcast(F32)[:, BANK * half : BANK * half + BANK].rearrange(
                            "p (g m u) -> p g m u", g=2, m=P, u=2
                        ),
                        in_=tp[:].rearrange("p (g u) m -> p g m u", g=2, u=2),
                    )


        def sort_blocks(engine_copy, k):
            bsort[k] = bsort_pool.tile([P, BLOCKS, 2, SQ], F32, name="bsort%d" % k, tag="bsort", align_bytes=64)
            words = braw[:, k].rearrange("p g r w -> p (g r w)").bitcast(F32)
            engine_copy(out=bsort[k][:].rearrange("p n u q -> p n q u"), in_=words.rearrange("p (n q u) -> p n q u", n=BLOCKS, u=2))

        def transpose_blocks(k):
            bturned[k] = btr_pool.tile([P, BLOCKS * 2 * SQ], F32, name="btr%d" % k, tag="btr", align_bytes=64)
            nc.vector.transpose(out=bturned[k][:], in_=bsort[k][:].rearrange("p n u q -> p (n u q)"))

        def regroup_blocks(k):
            regrouped = bgrp_pool.tile([P, CIN], BF16, name="bgrp%d" % k, tag="bgrp", align_bytes=64)
            wgrp[(FIRST_BLOCK_PAIR + k // 2, k % 2)] = regrouped
            nc.scalar.copy(
                out=regrouped[:].bitcast(F32).rearrange("p (n b u) -> p n b u", n=BLOCKS, u=2),
                in_=bturned[k][:].rearrange("p (n u b) -> p n b u", n=BLOCKS, u=2),
            )

        def block_step(j, b):
            turn = j - FIRST_TURN
            if not 0 <= turn < BLOCK_PANELS:
                return
            k = turn // 2 * 2
            if turn % 2 == 0:
                if b == 0:
                    sort_blocks(nc.vector.tensor_copy if j < PG_PAIRS else nc.scalar.copy, k)
                if b == 1:
                    sort_blocks(nc.scalar.copy, k + 1)
                    transpose_blocks(k)
            else:
                if b == 0:
                    transpose_blocks(k + 1)
                    regroup_blocks(k)
                if b == 2:
                    regroup_blocks(k + 1)

        def quantise_w(j):
            for s in range(2):
                wc[(j, s)] = wq_pool.tile([P, PASSES * P], U32, name="wc%d_%d" % (j, s), tag="wc", align_bytes=256)
                ws[(j, s)] = wq_pool.tile([P, PASSES * P], U8, name="ws%d_%d" % (j, s), tag="ws", align_bytes=256)
                nc.vector.quantize_mx(
                    out=wc[(j, s)][:].bitcast(FP8X4), scales=ws[(j, s)][:], in_=wgrp[(j, s)][:]
                )

        def job(j, b):
            for s in range(2):
                if s == 0 or (j, b) == LAST_JOB:
                    bank = acc_pool.tile([P, 2, HW], F32, name="acc%d_%d_%d" % (j, b, s), tag="acc")
                acc[(j, b, s)] = bank
                for g in range(PASSES):
                    nc.tensor.matmul_mx(
                        out=bank[:, s, :],
                        lhsT=wc[(j, s)][:, P * g : P * g + P].bitcast(FP8X4),
                        lhsT_scale=ws[(j, s)][:, P * g : P * g + P],
                        rhs=xc[b][:, HW * g : HW * g + HW].bitcast(FP8X4),
                        rhs_scale=xs[b][:, HW * g : HW * g + HW],
                        start=(g == 0),
                        stop=(g == PASSES - 1),
                    )

        def drain(j, b):
            bank = acc[(j, b, 0)]
            if j < PG_PAIRS:
                p_sb = small.tile([P, HW], F32, name="p_sb%d_%d" % (j, b), tag="p_sb")
                nc.scalar.copy(out=p_sb[:], in_=bank[:, 0, :])
                prod = small.tile([P, HW], F32, name="prod%d_%d" % (j, b), tag="prod")
                nc.vector.scalar_tensor_tensor(
                    out=prod[:],
                    in0=bank[:, 1, :],
                    scalar=1.0,
                    in1=p_sb[:],
                    op0=MULT,
                    op1=MULT,
                    accum_out=part[:, j * IMAGES + b : j * IMAGES + b + 1],
                )
            else:
                panel = 2 * (j - PG_PAIRS)
                c, a = panel // PPG, panel % PPG
                factor = att[:, c * IMAGES + b : c * IMAGES + b + 1]
                dst = out[b, c].rearrange("(p a) n -> p a n", a=PPG)
                if (j, b) == LAST_JOB:
                    y_first = small.tile([P, HW], F32, name="y_first", tag="y_first", bufs=1)
                    nc.vector.tensor_scalar(out=y_first[:], in0=bank[:, 0, :], scalar1=factor, scalar2=None, op0=MULT)
                    nc.sync.dma_start(out=dst[:, a, :], in_=y_first[:])
                    y_second = small.tile([P, HW], F32, name="y_second", tag="y_second", bufs=1)
                    nc.scalar.activation(out=y_second[:], in_=acc[(j, b, 1)][:, 1, :], func=COPY, scale=factor)
                    nc.sync.dma_start(out=dst[:, a + 1, :], in_=y_second[:])
                    return
                y_sb = small.tile([P, 2, HW], F32, name="y_sb%d_%d" % (j, b), tag="y_sb", bufs=6)
                if b != 1:
                    nc.scalar.activation(out=y_sb[:], in_=bank[:], func=COPY, scale=factor)
                else:
                    nc.vector.tensor_scalar(out=y_sb[:], in0=bank[:], scalar1=factor, scalar2=None, op0=MULT)
                nc.sync.dma_start(out=dst[:, a : a + 2, :], in_=y_sb[:])

        def attention(c):
            n = PPG * IMAGES
            att_ps = tp_pool.tile([P, 4, P], F32, name="att_ps%d" % c, tag="tp")
            sums = att_ps[:, 0, 0:n]
            nc.tensor.matmul(sums, lhsT=ones[:], rhs=part[:, n * c : n * c + n], start=True, stop=True)
            nc.vector.tensor_reduce(
                out=att[:, IMAGES * c : IMAGES * c + IMAGES],
                in_=sums.rearrange("p (a b) -> p b a", a=PPG, b=IMAGES),
                axis=mybir.AxisListType.X,
                op=ADD,
            )

        def run(jobs, between=None):
            for j, b in jobs:
                job(j, b)
            if between is not None:
                prep_x(between)
            for j, b in jobs:
                drain(j, b)

        def run(jobs, between=None):
            for j, b in jobs:
                job(j, b)
            if between is not None:
                prep_x(between)
            for j, b in jobs:
                drain(j, b)

        transposes(0)
        quantise_w(0)
        prep_x(0)
        for r in range(1, START_PAIRS + 1):
            transposes(r)
            quantise_w(r)
            if r >= SORT_FROM - 1:
                sort_words(r + 1)
            run([(j, r - 1) for j in range(r)], between=(r if r < IMAGES else None))
            if r < START_PAIRS:
                run([(r, b) for b in range(r)])
        for j in range(START_PAIRS, PAIRS):
            if j + 1 < FIRST_BLOCK_PAIR:
                transposes(j + 1)
            if j + 2 < FIRST_BLOCK_PAIR:
                sort_words(j + 2)
            if j >= PG_PAIRS and (j - PG_PAIRS) * 2 % PPG == 0:
                attention((j - PG_PAIRS) * 2 // PPG)
            if j + 1 < PAIRS:
                quantise_w(j + 1)
            for b in range(IMAGES):
                job(j, b)
                drain(j, b)
                block_step(j, b)
